import numpy as np
import ml_dtypes

BF16 = ml_dtypes.bfloat16


def bf(x):
    return np.asarray(x, np.float32).astype(BF16)


def f32(x):
    return np.asarray(x, np.float32)


def f64(x):
    return np.asarray(x).astype(np.float64)


def striped(idx):
    return np.tile(idx.reshape(-1, 16).T, (8, 1))


D, S, M, N = 128, 1024, 512, 512
DENS = 0.03125
WSCALE = 2.0


def setup_inputs():
    table = bf(np.random.standard_normal((D, S)))
    w0 = bf(WSCALE * np.random.standard_normal((D, M)) / np.sqrt(D))
    adj_t = bf(np.random.uniform(size=(N, N)) * (np.random.uniform(size=(N, N)) < DENS))
    b0 = f32(0.1 * np.random.standard_normal((M, 1)))
    return {"table": table, "w0": w0, "adj_t": adj_t, "b0": b0, "offs": striped(np.random.permutation(S)[:N])}


def reference(table, w0, adj_t, b0, offs):
    idx = offs[:16].T.reshape(-1)
    y = f64(w0).T @ f64(table)[:, idx]
    a = f64(adj_t)
    deg = 1.0 + a.sum(axis=0, keepdims=True)
    return np.maximum((y + y @ a) / deg + f64(b0), 0.0)

@@ -1,0 +1,90 @@
+import concourse.mybir as mybir
+from concourse.masks import make_identity
+
+BF16, F32, U16 = mybir.dt.bfloat16, mybir.dt.float32, mybir.dt.uint16
+RELU = mybir.ActivationFunctionType.Relu
+ADD, MULT = mybir.AluOpType.add, mybir.AluOpType.mult
+
+P = 128
+D, S, M, N = 128, 1024, 512, 512
+M_BLOCKS = M // P
+J_BLOCKS = N // P
+
+FLOPS = 2 * D * M * N + 2 * M * N * N
+
+
+def tile_gnnviasmetabolicas_kernel(tc, table, w0, adj_t, b0, offs, out):
+    nc = tc.nc
+    adj_blocks = adj_t.rearrange("(jb p) i -> jb p i", p=P)
+    out_blocks = out.rearrange("(mb p) i -> mb p i", p=P)
+
+    with (
+        tc.tile_pool(name="held", bufs=1) as held,
+        tc.tile_pool(name="work", bufs=2) as work,
+        tc.psum_pool(name="psum_acc", bufs=5) as psum_acc,
+        tc.psum_pool(name="psum_t", bufs=2) as psum_t,
+        tc.psum_pool(name="psum_deg", bufs=1) as psum_deg,
+    ):
+        offsets = held.tile([P, N // 16], U16, name="offsets")
+        nc.sync.dma_start(offsets[:], offs)
+        table_sb = held.tile([P, S], BF16, name="table_sb")
+        nc.sync.dma_start(table_sb[:], table)
+        w0_sb = held.tile([P, M], BF16, name="w0_sb")
+        nc.scalar.dma_start(w0_sb[:], w0)
+        adj_sb = [held.tile([P, N], BF16, name=f"adj_sb{jb}") for jb in range(J_BLOCKS)]
+        for jb in range(J_BLOCKS):
+            queue = nc.sync if jb % 2 == 0 else nc.scalar
+            queue.dma_start(adj_sb[jb][:], adj_blocks[jb])
+        b0_sb = held.tile([P, M_BLOCKS], F32, name="b0_sb")
+        with nc.allow_non_contiguous_dma(reason="512 floats, one to a partition and block"):
+            nc.gpsimd.dma_start(b0_sb[:], b0.rearrange("(mb p) one -> p (mb one)", p=P))
+
+        identity = held.tile([P, P], BF16, name="identity")
+        make_identity(nc, identity[:])
+        ones = held.tile([P, P], BF16, name="ones")
+        nc.vector.memset(ones[:], 1.0)
+
+        y_f32 = []
+        y_bf16 = []
+        for mb in range(M_BLOCKS):
+            y_ps = psum_acc.tile([P, N], F32, name="y_ps", tag="acc")
+            nc.tensor.matmul(y_ps[:], w0_sb[:, mb * P : (mb + 1) * P], table_sb[:].indirect(offsets[:]))
+            y_f32.append(held.tile([P, N], F32, name=f"y_f32_{mb}"))
+            nc.scalar.copy(y_f32[mb][:], y_ps[:])
+            y_bf16.append(held.tile([P, N], BF16, name=f"y_bf16_{mb}"))
+            nc.vector.tensor_copy(y_bf16[mb][:], y_f32[mb][:])
+
+        deg_ps = psum_deg.tile([P, N], F32, name="deg_ps")
+        for jb in range(J_BLOCKS):
+            nc.tensor.matmul(deg_ps[:], ones[:], adj_sb[jb][:], start=(jb == 0), stop=(jb == J_BLOCKS - 1))
+        deg = held.tile([P, N], F32, name="deg")
+        nc.vector.tensor_scalar_add(deg[:], deg_ps[:], 1.0)
+        inv_deg = held.tile([P, N], F32, name="inv_deg")
+        nc.vector.reciprocal(inv_deg[:], deg[:])
+
+        y_t = []
+        for mb in range(M_BLOCKS):
+            y_t_ps = psum_t.tile([P, N], BF16, name="y_t_ps")
+            for jb in range(J_BLOCKS):
+                block = slice(jb * P, (jb + 1) * P)
+                nc.tensor.transpose(y_t_ps[:, block], y_bf16[mb][:, block], identity[:])
+            y_t.append(held.tile([P, N], BF16, name=f"y_t{mb}"))
+            nc.scalar.copy(y_t[mb][:], y_t_ps[:])
+
+        for mb in range(M_BLOCKS):
+            agg_ps = psum_acc.tile([P, N], F32, name="agg_ps", tag="acc")
+            for jb in range(J_BLOCKS):
+                nc.tensor.matmul(
+                    agg_ps[:],
+                    y_t[mb][:, jb * P : (jb + 1) * P],
+                    adj_sb[jb][:],
+                    start=(jb == 0),
+                    stop=(jb == J_BLOCKS - 1),
+                )
+            total = work.tile([P, N], F32, name="total")
+            nc.vector.tensor_tensor(total[:], agg_ps[:], y_f32[mb][:], ADD)
+            mean = work.tile([P, N], F32, name="mean")
+            nc.vector.tensor_tensor(mean[:], total[:], inv_deg[:], MULT)
+            result = work.tile([P, N], F32, name="result")
+            nc.scalar.activation(result[:], mean[:], RELU, bias=b0_sb[:, mb : mb + 1])
+            nc.sync.dma_start(out_blocks[mb], result[:])

@@ -9,6 +9,7 @@ P = 128
 D, S, M, N = 128, 1024, 512, 512
 M_BLOCKS = M // P
 J_BLOCKS = N // P
+I_BLOCKS = N // P
 
 FLOPS = 2 * D * M * N + 2 * M * N * N
 
@@ -21,7 +22,7 @@ def tile_gnnviasmetabolicas_kernel(tc, table, w0, adj_t, b0, offs, out):
     with (
         tc.tile_pool(name="held", bufs=1) as held,
         tc.tile_pool(name="work", bufs=2) as work,
-        tc.psum_pool(name="psum_acc", bufs=5) as psum_acc,
+        tc.psum_pool(name="psum_acc", bufs=4) as psum_acc,
         tc.psum_pool(name="psum_t", bufs=2) as psum_t,
         tc.psum_pool(name="psum_deg", bufs=1) as psum_deg,
     ):
@@ -39,10 +40,12 @@ def tile_gnnviasmetabolicas_kernel(tc, table, w0, adj_t, b0, offs, out):
         with nc.allow_non_contiguous_dma(reason="512 floats, one to a partition and block"):
             nc.gpsimd.dma_start(b0_sb[:], b0.rearrange("(mb p) one -> p (mb one)", p=P))
 
+        identity_f32 = held.tile([P, P], F32, name="identity_f32")
+        make_identity(nc, identity_f32[:])
         identity = held.tile([P, P], BF16, name="identity")
-        make_identity(nc, identity[:])
-        ones = held.tile([P, P], BF16, name="ones")
-        nc.vector.memset(ones[:], 1.0)
+        nc.vector.tensor_copy(identity[:], identity_f32[:])
+        ones_col = held.tile([P, 1], BF16, name="ones_col")
+        nc.vector.memset(ones_col[:], 1.0)
 
         y_f32 = []
         y_bf16 = []
@@ -54,13 +57,25 @@ def tile_gnnviasmetabolicas_kernel(tc, table, w0, adj_t, b0, offs, out):
             y_bf16.append(held.tile([P, N], BF16, name=f"y_bf16_{mb}"))
             nc.vector.tensor_copy(y_bf16[mb][:], y_f32[mb][:])
 
-        deg_ps = psum_deg.tile([P, N], F32, name="deg_ps")
-        for jb in range(J_BLOCKS):
-            nc.tensor.matmul(deg_ps[:], ones[:], adj_sb[jb][:], start=(jb == 0), stop=(jb == J_BLOCKS - 1))
-        deg = held.tile([P, N], F32, name="deg")
-        nc.vector.tensor_scalar_add(deg[:], deg_ps[:], 1.0)
-        inv_deg = held.tile([P, N], F32, name="inv_deg")
-        nc.vector.reciprocal(inv_deg[:], deg[:])
+        deg_ps = psum_deg.tile([P, I_BLOCKS], F32, name="deg_ps")
+        for ib in range(I_BLOCKS):
+            for jb in range(J_BLOCKS):
+                nc.tensor.matmul(
+                    deg_ps[:, ib : ib + 1],
+                    adj_sb[jb][:, ib * P : (ib + 1) * P],
+                    ones_col[:],
+                    start=(jb == 0),
+                    stop=(jb == J_BLOCKS - 1),
+                )
+        deg_col = held.tile([P, I_BLOCKS], F32, name="deg_col")
+        nc.vector.tensor_scalar_add(deg_col[:], deg_ps[:], 1.0)
+        inv_col = held.tile([P, I_BLOCKS], F32, name="inv_col")
+        nc.vector.reciprocal(inv_col[:], deg_col[:])
+        inv_rep = held.tile([P, I_BLOCKS, P], F32, name="inv_rep")
+        nc.vector.tensor_copy(inv_rep[:], inv_col[:].unsqueeze(2).to_broadcast([P, I_BLOCKS, P]))
+        inv_deg = psum_deg.tile([P, N], F32, name="inv_deg")
+        for ib in range(I_BLOCKS):
+            nc.tensor.transpose(inv_deg[:, ib * P : (ib + 1) * P], inv_rep[:, ib, :], identity_f32[:])
 
         y_t = []
         for mb in range(M_BLOCKS):

@@ -11,6 +11,8 @@ M_BLOCKS = M // P
 J_BLOCKS = N // P
 I_BLOCKS = N // P
 
+WARM_UP_COLUMNS = 2048
+
 FLOPS = 2 * D * M * N + 2 * M * N * N
 
 
@@ -21,9 +23,9 @@ def tile_gnnviasmetabolicas_kernel(tc, table, w0, adj_t, b0, offs, out):
 
     with (
         tc.tile_pool(name="held", bufs=1) as held,
-        tc.tile_pool(name="work", bufs=2) as work,
+        tc.tile_pool(name="work", bufs=M_BLOCKS) as work,
         tc.psum_pool(name="psum_acc", bufs=4) as psum_acc,
-        tc.psum_pool(name="psum_t", bufs=2) as psum_t,
+        tc.psum_pool(name="psum_t", bufs=3) as psum_t,
         tc.psum_pool(name="psum_deg", bufs=1) as psum_deg,
     ):
         offsets = held.tile([P, N // 16], U16, name="offsets")
@@ -38,7 +40,13 @@ def tile_gnnviasmetabolicas_kernel(tc, table, w0, adj_t, b0, offs, out):
             queue.dma_start(adj_sb[jb][:], adj_blocks[jb])
         b0_sb = held.tile([P, M_BLOCKS], F32, name="b0_sb")
         with nc.allow_non_contiguous_dma(reason="512 floats, one to a partition and block"):
-            nc.gpsimd.dma_start(b0_sb[:], b0.rearrange("(mb p) one -> p (mb one)", p=P))
+            nc.sync.dma_start(b0_sb[:], b0.rearrange("(mb p) one -> p (mb one)", p=P))
+
+        zeros = held.tile([P, N], BF16, name="zeros")
+        nc.gpsimd.memset(zeros[:], 0.0)
+        warm_ps = psum_acc.tile([P, N], F32, name="warm_ps", tag="acc")
+        for step in range(WARM_UP_COLUMNS // N):
+            nc.tensor.matmul(warm_ps[:], zeros[:, 0:P], zeros[:])
 
         identity_f32 = held.tile([P, P], F32, name="identity_f32")
         make_identity(nc, identity_f32[:])
@@ -47,17 +55,21 @@ def tile_gnnviasmetabolicas_kernel(tc, table, w0, adj_t, b0, offs, out):
         ones_col = held.tile([P, 1], BF16, name="ones_col")
         nc.vector.memset(ones_col[:], 1.0)
 
+        act_warm = held.tile([P, 1], F32, name="act_warm")
+        nc.vector.memset(act_warm[:], 0.0)
+        nc.scalar.activation(act_warm[:], act_warm[:], RELU)
+
         y_f32 = []
         y_bf16 = []
         for mb in range(M_BLOCKS):
             y_ps = psum_acc.tile([P, N], F32, name="y_ps", tag="acc")
             nc.tensor.matmul(y_ps[:], w0_sb[:, mb * P : (mb + 1) * P], table_sb[:].indirect(offsets[:]))
+            y_bf16.append(held.tile([P, N], BF16, name=f"y_bf16_{mb}"))
+            nc.vector.tensor_copy(y_bf16[mb][:], y_ps[:])
             y_f32.append(held.tile([P, N], F32, name=f"y_f32_{mb}"))
             nc.scalar.copy(y_f32[mb][:], y_ps[:])
-            y_bf16.append(held.tile([P, N], BF16, name=f"y_bf16_{mb}"))
-            nc.vector.tensor_copy(y_bf16[mb][:], y_f32[mb][:])
 
-        deg_ps = psum_deg.tile([P, I_BLOCKS], F32, name="deg_ps")
+        deg_ps = psum_deg.tile([P, I_BLOCKS], F32, name="deg_ps", tag="deg")
         for ib in range(I_BLOCKS):
             for jb in range(J_BLOCKS):
                 nc.tensor.matmul(
@@ -72,10 +84,7 @@ def tile_gnnviasmetabolicas_kernel(tc, table, w0, adj_t, b0, offs, out):
         inv_col = held.tile([P, I_BLOCKS], F32, name="inv_col")
         nc.vector.reciprocal(inv_col[:], deg_col[:])
         inv_rep = held.tile([P, I_BLOCKS, P], F32, name="inv_rep")
-        nc.vector.tensor_copy(inv_rep[:], inv_col[:].unsqueeze(2).to_broadcast([P, I_BLOCKS, P]))
-        inv_deg = psum_deg.tile([P, N], F32, name="inv_deg")
-        for ib in range(I_BLOCKS):
-            nc.tensor.transpose(inv_deg[:, ib * P : (ib + 1) * P], inv_rep[:, ib, :], identity_f32[:])
+        nc.gpsimd.tensor_copy(inv_rep[:], inv_col[:].unsqueeze(2).to_broadcast([P, I_BLOCKS, P]))
 
         y_t = []
         for mb in range(M_BLOCKS):
@@ -84,7 +93,11 @@ def tile_gnnviasmetabolicas_kernel(tc, table, w0, adj_t, b0, offs, out):
                 block = slice(jb * P, (jb + 1) * P)
                 nc.tensor.transpose(y_t_ps[:, block], y_bf16[mb][:, block], identity[:])
             y_t.append(held.tile([P, N], BF16, name=f"y_t{mb}"))
-            nc.scalar.copy(y_t[mb][:], y_t_ps[:])
+            nc.vector.tensor_copy(y_t[mb][:], y_t_ps[:])
+
+        inv_deg = psum_deg.tile([P, N], F32, name="inv_deg", tag="deg")
+        for ib in range(I_BLOCKS):
+            nc.tensor.transpose(inv_deg[:, ib * P : (ib + 1) * P], inv_rep[:, ib, :], identity_f32[:])
 
         for mb in range(M_BLOCKS):
             agg_ps = psum_acc.tile([P, N], F32, name="agg_ps", tag="acc")

@@ -3,15 +3,12 @@ from concourse.masks import make_identity
 
 BF16, F32, U16 = mybir.dt.bfloat16, mybir.dt.float32, mybir.dt.uint16
 RELU = mybir.ActivationFunctionType.Relu
-ADD, MULT = mybir.AluOpType.add, mybir.AluOpType.mult
+MULT = mybir.AluOpType.mult
 
 P = 128
 D, S, M, N = 128, 1024, 512, 512
 M_BLOCKS = M // P
 J_BLOCKS = N // P
-I_BLOCKS = N // P
-
-WARM_UP_COLUMNS = 2048
 
 FLOPS = 2 * D * M * N + 2 * M * N * N
 
@@ -24,95 +21,73 @@ def tile_gnnviasmetabolicas_kernel(tc, table, w0, adj_t, b0, offs, out):
     with (
         tc.tile_pool(name="held", bufs=1) as held,
         tc.tile_pool(name="work", bufs=M_BLOCKS) as work,
-        tc.psum_pool(name="psum_acc", bufs=4) as psum_acc,
-        tc.psum_pool(name="psum_t", bufs=3) as psum_t,
-        tc.psum_pool(name="psum_deg", bufs=1) as psum_deg,
+        tc.psum_pool(name="psum_sum", bufs=M_BLOCKS) as psum_sum,
+        tc.psum_pool(name="psum_tmp", bufs=4) as psum_tmp,
     ):
+        adj_sb = [held.tile([P, N], BF16, name=f"adj_sb{jb}") for jb in range(J_BLOCKS)]
+        for jb in range(J_BLOCKS):
+            queue = nc.sync if jb % 2 == 0 else nc.scalar
+            queue.dma_start(adj_sb[jb][:], adj_blocks[jb])
         offsets = held.tile([P, N // 16], U16, name="offsets")
         nc.sync.dma_start(offsets[:], offs)
         table_sb = held.tile([P, S], BF16, name="table_sb")
         nc.sync.dma_start(table_sb[:], table)
         w0_sb = held.tile([P, M], BF16, name="w0_sb")
         nc.scalar.dma_start(w0_sb[:], w0)
-        adj_sb = [held.tile([P, N], BF16, name=f"adj_sb{jb}") for jb in range(J_BLOCKS)]
-        for jb in range(J_BLOCKS):
-            queue = nc.sync if jb % 2 == 0 else nc.scalar
-            queue.dma_start(adj_sb[jb][:], adj_blocks[jb])
         b0_sb = held.tile([P, M_BLOCKS], F32, name="b0_sb")
         with nc.allow_non_contiguous_dma(reason="512 floats, one to a partition and block"):
             nc.sync.dma_start(b0_sb[:], b0.rearrange("(mb p) one -> p (mb one)", p=P))
 
-        zeros = held.tile([P, N], BF16, name="zeros")
-        nc.gpsimd.memset(zeros[:], 0.0)
-        warm_ps = psum_acc.tile([P, N], F32, name="warm_ps", tag="acc")
-        for step in range(WARM_UP_COLUMNS // N):
-            nc.tensor.matmul(warm_ps[:], zeros[:, 0:P], zeros[:])
-
-        identity_f32 = held.tile([P, P], F32, name="identity_f32")
-        make_identity(nc, identity_f32[:])
+        ones = held.tile([P, P], BF16, name="ones")
+        nc.vector.memset(ones[:], 1.0)
         identity = held.tile([P, P], BF16, name="identity")
-        nc.vector.tensor_copy(identity[:], identity_f32[:])
-        ones_col = held.tile([P, 1], BF16, name="ones_col")
-        nc.vector.memset(ones_col[:], 1.0)
+        make_identity(nc, identity[:])
 
-        act_warm = held.tile([P, 1], F32, name="act_warm")
-        nc.vector.memset(act_warm[:], 0.0)
-        nc.scalar.activation(act_warm[:], act_warm[:], RELU)
+        deg_ps = psum_tmp.tile([P, N], F32, name="deg_ps", tag="tmp")
+        for jb in range(J_BLOCKS):
+            nc.tensor.matmul(deg_ps[:], ones[:], adj_sb[jb][:], start=(jb == 0), stop=(jb == J_BLOCKS - 1))
+        deg = held.tile([P, N], F32, name="deg")
+        nc.vector.tensor_scalar_add(deg[:], deg_ps[:], 1.0)
+        inv_deg = held.tile([P, N], F32, name="inv_deg")
+        nc.vector.reciprocal(inv_deg[:], deg[:])
 
-        y_f32 = []
         y_bf16 = []
         for mb in range(M_BLOCKS):
-            y_ps = psum_acc.tile([P, N], F32, name="y_ps", tag="acc")
+            y_ps = psum_tmp.tile([P, N], F32, name="y_ps", tag="tmp")
             nc.tensor.matmul(y_ps[:], w0_sb[:, mb * P : (mb + 1) * P], table_sb[:].indirect(offsets[:]))
             y_bf16.append(held.tile([P, N], BF16, name=f"y_bf16_{mb}"))
-            nc.vector.tensor_copy(y_bf16[mb][:], y_ps[:])
-            y_f32.append(held.tile([P, N], F32, name=f"y_f32_{mb}"))
-            nc.scalar.copy(y_f32[mb][:], y_ps[:])
-
-        deg_ps = psum_deg.tile([P, I_BLOCKS], F32, name="deg_ps", tag="deg")
-        for ib in range(I_BLOCKS):
-            for jb in range(J_BLOCKS):
-                nc.tensor.matmul(
-                    deg_ps[:, ib : ib + 1],
-                    adj_sb[jb][:, ib * P : (ib + 1) * P],
-                    ones_col[:],
-                    start=(jb == 0),
-                    stop=(jb == J_BLOCKS - 1),
-                )
-        deg_col = held.tile([P, I_BLOCKS], F32, name="deg_col")
-        nc.vector.tensor_scalar_add(deg_col[:], deg_ps[:], 1.0)
-        inv_col = held.tile([P, I_BLOCKS], F32, name="inv_col")
-        nc.vector.reciprocal(inv_col[:], deg_col[:])
-        inv_rep = held.tile([P, I_BLOCKS, P], F32, name="inv_rep")
-        nc.gpsimd.tensor_copy(inv_rep[:], inv_col[:].unsqueeze(2).to_broadcast([P, I_BLOCKS, P]))
+            nc.scalar.copy(y_bf16[mb][:], y_ps[:])
+        sum_ps = []
+        for mb in range(M_BLOCKS):
+            sum_ps.append(psum_sum.tile([P, N], F32, name="sum_ps"))
+            nc.tensor.matmul(
+                sum_ps[mb][:],
+                w0_sb[:, mb * P : (mb + 1) * P],
+                table_sb[:].indirect(offsets[:]),
+                start=True,
+                stop=False,
+            )
 
         y_t = []
         for mb in range(M_BLOCKS):
-            y_t_ps = psum_t.tile([P, N], BF16, name="y_t_ps")
+            y_t_ps = psum_tmp.tile([P, N], BF16, name="y_t_ps", tag="tmp")
             for jb in range(J_BLOCKS):
                 block = slice(jb * P, (jb + 1) * P)
                 nc.tensor.transpose(y_t_ps[:, block], y_bf16[mb][:, block], identity[:])
             y_t.append(held.tile([P, N], BF16, name=f"y_t{mb}"))
-            nc.vector.tensor_copy(y_t[mb][:], y_t_ps[:])
-
-        inv_deg = psum_deg.tile([P, N], F32, name="inv_deg", tag="deg")
-        for ib in range(I_BLOCKS):
-            nc.tensor.transpose(inv_deg[:, ib * P : (ib + 1) * P], inv_rep[:, ib, :], identity_f32[:])
+            nc.scalar.copy(y_t[mb][:], y_t_ps[:])
 
         for mb in range(M_BLOCKS):
-            agg_ps = psum_acc.tile([P, N], F32, name="agg_ps", tag="acc")
             for jb in range(J_BLOCKS):
                 nc.tensor.matmul(
-                    agg_ps[:],
+                    sum_ps[mb][:],
                     y_t[mb][:, jb * P : (jb + 1) * P],
                     adj_sb[jb][:],
-                    start=(jb == 0),
+                    start=False,
                     stop=(jb == J_BLOCKS - 1),
                 )
-            total = work.tile([P, N], F32, name="total")
-            nc.vector.tensor_tensor(total[:], agg_ps[:], y_f32[mb][:], ADD)
             mean = work.tile([P, N], F32, name="mean")
-            nc.vector.tensor_tensor(mean[:], total[:], inv_deg[:], MULT)
+            nc.vector.tensor_tensor(mean[:], sum_ps[mb][:], inv_deg[:], MULT)
             result = work.tile([P, N], F32, name="result")
             nc.scalar.activation(result[:], mean[:], RELU, bias=b0_sb[:, mb : mb + 1])
             nc.sync.dma_start(out_blocks[mb], result[:])

@@ -70,10 +70,10 @@ def tile_gnnviasmetabolicas_kernel(tc, table, w0, adj_t, b0, offs, out):
 
         y_t = []
         for mb in range(M_BLOCKS):
-            y_t_ps = psum_tmp.tile([P, N], BF16, name="y_t_ps", tag="tmp")
+            y_t_ps = psum_tmp.tile([P, N], F32, name="y_t_ps", tag="tmp")
             for jb in range(J_BLOCKS):
                 block = slice(jb * P, (jb + 1) * P)
-                nc.tensor.transpose(y_t_ps[:, block], y_bf16[mb][:, block], identity[:])
+                nc.tensor.matmul(y_t_ps[:, block], y_bf16[mb][:, block], identity[:])
             y_t.append(held.tile([P, N], BF16, name=f"y_t{mb}"))
             nc.scalar.copy(y_t[mb][:], y_t_ps[:])
 

@@ -70,10 +70,10 @@ def tile_gnnviasmetabolicas_kernel(tc, table, w0, adj_t, b0, offs, out):
 
         y_t = []
         for mb in range(M_BLOCKS):
-            y_t_ps = psum_tmp.tile([P, N], F32, name="y_t_ps", tag="tmp")
+            y_t_ps = psum_tmp.tile([P, N], BF16, name="y_t_ps", tag="tmp")
             for jb in range(J_BLOCKS):
                 block = slice(jb * P, (jb + 1) * P)
-                nc.tensor.matmul(y_t_ps[:, block], y_bf16[mb][:, block], identity[:])
+                nc.tensor.transpose(y_t_ps[:, block], y_bf16[mb][:, block], identity[:])
             y_t.append(held.tile([P, N], BF16, name=f"y_t{mb}"))
             nc.scalar.copy(y_t[mb][:], y_t_ps[:])
 
@@ -87,7 +87,9 @@ def tile_gnnviasmetabolicas_kernel(tc, table, w0, adj_t, b0, offs, out):
                     stop=(jb == J_BLOCKS - 1),
                 )
             mean = work.tile([P, N], F32, name="mean")
-            nc.vector.tensor_tensor(mean[:], sum_ps[mb][:], inv_deg[:], MULT)
             result = work.tile([P, N], F32, name="result")
-            nc.scalar.activation(result[:], mean[:], RELU, bias=b0_sb[:, mb : mb + 1])
-            nc.sync.dma_start(out_blocks[mb], result[:])
+            for half in range(2):
+                cols = slice(half * (N // 2), (half + 1) * (N // 2))
+                nc.vector.tensor_tensor(mean[:, cols], sum_ps[mb][:, cols], inv_deg[:, cols], MULT)
+                nc.scalar.activation(result[:, cols], mean[:, cols], RELU, bias=b0_sb[:, mb : mb + 1])
+                nc.sync.dma_start(out_blocks[mb][:, cols], result[:, cols])

@@ -3,12 +3,13 @@ from concourse.masks import make_identity
 
 BF16, F32, U16 = mybir.dt.bfloat16, mybir.dt.float32, mybir.dt.uint16
 RELU = mybir.ActivationFunctionType.Relu
-MULT = mybir.AluOpType.mult
+ADD, MULT = mybir.AluOpType.add, mybir.AluOpType.mult
 
 P = 128
 D, S, M, N = 128, 1024, 512, 512
 M_BLOCKS = M // P
 J_BLOCKS = N // P
+PSUM_BANKS = 8
 
 FLOPS = 2 * D * M * N + 2 * M * N * N
 
@@ -20,9 +21,10 @@ def tile_gnnviasmetabolicas_kernel(tc, table, w0, adj_t, b0, offs, out):
 
     with (
         tc.tile_pool(name="held", bufs=1) as held,
+        tc.tile_pool(name="y_sb", bufs=M_BLOCKS) as y_sb,
         tc.tile_pool(name="work", bufs=M_BLOCKS) as work,
-        tc.psum_pool(name="psum_sum", bufs=M_BLOCKS) as psum_sum,
-        tc.psum_pool(name="psum_tmp", bufs=4) as psum_tmp,
+        tc.psum_pool(name="psum_y", bufs=M_BLOCKS) as psum_y,
+        tc.psum_pool(name="psum", bufs=PSUM_BANKS - M_BLOCKS) as psum,
     ):
         adj_sb = [held.tile([P, N], BF16, name=f"adj_sb{jb}") for jb in range(J_BLOCKS)]
         for jb in range(J_BLOCKS):
@@ -43,7 +45,7 @@ def tile_gnnviasmetabolicas_kernel(tc, table, w0, adj_t, b0, offs, out):
         identity = held.tile([P, P], BF16, name="identity")
         make_identity(nc, identity[:])
 
-        deg_ps = psum_tmp.tile([P, N], F32, name="deg_ps", tag="tmp")
+        deg_ps = psum.tile([P, N], F32, name="deg_ps", tag="bank")
         for jb in range(J_BLOCKS):
             nc.tensor.matmul(deg_ps[:], ones[:], adj_sb[jb][:], start=(jb == 0), stop=(jb == J_BLOCKS - 1))
         deg = held.tile([P, N], F32, name="deg")
@@ -51,45 +53,40 @@ def tile_gnnviasmetabolicas_kernel(tc, table, w0, adj_t, b0, offs, out):
         inv_deg = held.tile([P, N], F32, name="inv_deg")
         nc.vector.reciprocal(inv_deg[:], deg[:])
 
-        y_bf16 = []
+        y_ps, y_bf16 = [], []
         for mb in range(M_BLOCKS):
-            y_ps = psum_tmp.tile([P, N], F32, name="y_ps", tag="tmp")
-            nc.tensor.matmul(y_ps[:], w0_sb[:, mb * P : (mb + 1) * P], table_sb[:].indirect(offsets[:]))
-            y_bf16.append(held.tile([P, N], BF16, name=f"y_bf16_{mb}"))
-            nc.scalar.copy(y_bf16[mb][:], y_ps[:])
-        sum_ps = []
-        for mb in range(M_BLOCKS):
-            sum_ps.append(psum_sum.tile([P, N], F32, name="sum_ps"))
-            nc.tensor.matmul(
-                sum_ps[mb][:],
-                w0_sb[:, mb * P : (mb + 1) * P],
-                table_sb[:].indirect(offsets[:]),
-                start=True,
-                stop=False,
-            )
+            y_ps.append(psum_y.tile([P, N], F32, name="y_ps"))
+            nc.tensor.matmul(y_ps[mb][:], w0_sb[:, mb * P : (mb + 1) * P], table_sb[:].indirect(offsets[:]))
+            y_bf16.append(y_sb.tile([P, N], BF16, name=f"y_bf16_{mb}", tag="y"))
+            nc.scalar.copy(y_bf16[mb][:], y_ps[mb][:])
 
-        y_t = []
+        y_t, y_f32 = [], []
         for mb in range(M_BLOCKS):
-            y_t_ps = psum_tmp.tile([P, N], BF16, name="y_t_ps", tag="tmp")
+            y_t_ps = psum.tile([P, N], BF16, name="y_t_ps", tag="bank")
             for jb in range(J_BLOCKS):
                 block = slice(jb * P, (jb + 1) * P)
                 nc.tensor.transpose(y_t_ps[:, block], y_bf16[mb][:, block], identity[:])
             y_t.append(held.tile([P, N], BF16, name=f"y_t{mb}"))
             nc.scalar.copy(y_t[mb][:], y_t_ps[:])
+            y_f32.append(y_sb.tile([P, N], F32, name=f"y_f32_{mb}", tag="y"))
+            nc.scalar.copy(y_f32[mb][:], y_ps[mb][:])
 
         for mb in range(M_BLOCKS):
+            sum_ps = psum.tile([P, N], F32, name="sum_ps", tag="bank")
             for jb in range(J_BLOCKS):
                 nc.tensor.matmul(
-                    sum_ps[mb][:],
+                    sum_ps[:],
                     y_t[mb][:, jb * P : (jb + 1) * P],
                     adj_sb[jb][:],
-                    start=False,
+                    start=(jb == 0),
                     stop=(jb == J_BLOCKS - 1),
                 )
+            total = work.tile([P, N], F32, name="total")
             mean = work.tile([P, N], F32, name="mean")
             result = work.tile([P, N], F32, name="result")
             for half in range(2):
                 cols = slice(half * (N // 2), (half + 1) * (N // 2))
-                nc.vector.tensor_tensor(mean[:, cols], sum_ps[mb][:, cols], inv_deg[:, cols], MULT)
+                nc.vector.tensor_tensor(total[:, cols], sum_ps[:, cols], y_f32[mb][:, cols], ADD)
+                nc.vector.tensor_tensor(mean[:, cols], total[:, cols], inv_deg[:, cols], MULT)
                 nc.scalar.activation(result[:, cols], mean[:, cols], RELU, bias=b0_sb[:, mb : mb + 1])
                 nc.sync.dma_start(out_blocks[mb][:, cols], result[:, cols])

@@ -9,6 +9,7 @@ P = 128
 D, S, M, N = 128, 1024, 512, 512
 M_BLOCKS = M // P
 J_BLOCKS = N // P
+LAST = M_BLOCKS - 1
 PSUM_BANKS = 8
 
 FLOPS = 2 * D * M * N + 2 * M * N * N
@@ -23,8 +24,7 @@ def tile_gnnviasmetabolicas_kernel(tc, table, w0, adj_t, b0, offs, out):
         tc.tile_pool(name="held", bufs=1) as held,
         tc.tile_pool(name="y_sb", bufs=M_BLOCKS) as y_sb,
         tc.tile_pool(name="work", bufs=M_BLOCKS) as work,
-        tc.psum_pool(name="psum_y", bufs=M_BLOCKS) as psum_y,
-        tc.psum_pool(name="psum", bufs=PSUM_BANKS - M_BLOCKS) as psum,
+        tc.psum_pool(name="psum", bufs=PSUM_BANKS) as psum,
     ):
         adj_sb = [held.tile([P, N], BF16, name=f"adj_sb{jb}") for jb in range(J_BLOCKS)]
         for jb in range(J_BLOCKS):
@@ -55,38 +55,56 @@ def tile_gnnviasmetabolicas_kernel(tc, table, w0, adj_t, b0, offs, out):
 
         y_ps, y_bf16 = [], []
         for mb in range(M_BLOCKS):
-            y_ps.append(psum_y.tile([P, N], F32, name="y_ps"))
+            y_ps.append(psum.tile([P, N], F32, name=f"y_ps{mb}", tag="bank"))
             nc.tensor.matmul(y_ps[mb][:], w0_sb[:, mb * P : (mb + 1) * P], table_sb[:].indirect(offsets[:]))
             y_bf16.append(y_sb.tile([P, N], BF16, name=f"y_bf16_{mb}", tag="y"))
             nc.scalar.copy(y_bf16[mb][:], y_ps[mb][:])
+        last_sum_ps = psum.tile([P, N], F32, name="last_sum_ps", tag="bank")
+        nc.tensor.matmul(
+            last_sum_ps[:],
+            w0_sb[:, LAST * P : (LAST + 1) * P],
+            table_sb[:].indirect(offsets[:]),
+            start=True,
+            stop=False,
+        )
 
         y_t, y_f32 = [], []
         for mb in range(M_BLOCKS):
-            y_t_ps = psum.tile([P, N], BF16, name="y_t_ps", tag="bank")
+            if mb % 2 == 0:
+                y_t_ps = psum.tile([P, 2 * N], BF16, name="y_t_ps", tag="bank")
+            in_bank = (mb % 2) * N
             for jb in range(J_BLOCKS):
-                block = slice(jb * P, (jb + 1) * P)
-                nc.tensor.transpose(y_t_ps[:, block], y_bf16[mb][:, block], identity[:])
+                nc.tensor.transpose(
+                    y_t_ps[:, in_bank + jb * P : in_bank + (jb + 1) * P], y_bf16[mb][:, jb * P : (jb + 1) * P], identity[:]
+                )
             y_t.append(held.tile([P, N], BF16, name=f"y_t{mb}"))
-            nc.scalar.copy(y_t[mb][:], y_t_ps[:])
-            y_f32.append(y_sb.tile([P, N], F32, name=f"y_f32_{mb}", tag="y"))
-            nc.scalar.copy(y_f32[mb][:], y_ps[mb][:])
+            nc.scalar.copy(y_t[mb][:], y_t_ps[:, in_bank : in_bank + N])
+            if mb != LAST:
+                y_f32.append(y_sb.tile([P, N], F32, name=f"y_f32_{mb}", tag="y"))
+                if mb < M_BLOCKS // 2:
+                    nc.vector.tensor_copy(y_f32[mb][:], y_ps[mb][:])
+                else:
+                    nc.scalar.copy(y_f32[mb][:], y_ps[mb][:])
 
         for mb in range(M_BLOCKS):
-            sum_ps = psum.tile([P, N], F32, name="sum_ps", tag="bank")
+            sum_ps = last_sum_ps if mb == LAST else psum.tile([P, N], F32, name="sum_ps", tag="bank")
             for jb in range(J_BLOCKS):
                 nc.tensor.matmul(
                     sum_ps[:],
                     y_t[mb][:, jb * P : (jb + 1) * P],
                     adj_sb[jb][:],
-                    start=(jb == 0),
+                    start=(jb == 0 and mb != LAST),
                     stop=(jb == J_BLOCKS - 1),
                 )
-            total = work.tile([P, N], F32, name="total")
             mean = work.tile([P, N], F32, name="mean")
             result = work.tile([P, N], F32, name="result")
             for half in range(2):
                 cols = slice(half * (N // 2), (half + 1) * (N // 2))
-                nc.vector.tensor_tensor(total[:, cols], sum_ps[:, cols], y_f32[mb][:, cols], ADD)
-                nc.vector.tensor_tensor(mean[:, cols], total[:, cols], inv_deg[:, cols], MULT)
+                if mb == LAST:
+                    nc.vector.tensor_tensor(mean[:, cols], sum_ps[:, cols], inv_deg[:, cols], MULT)
+                else:
+                    total = work.tile([P, N // 2], F32, name="total")
+                    nc.vector.tensor_tensor(total[:], sum_ps[:, cols], y_f32[mb][:, cols], ADD)
+                    nc.vector.tensor_tensor(mean[:, cols], total[:], inv_deg[:, cols], MULT)
                 nc.scalar.activation(result[:, cols], mean[:, cols], RELU, bias=b0_sb[:, mb : mb + 1])
                 nc.sync.dma_start(out_blocks[mb][:, cols], result[:, cols])

@@ -68,17 +68,18 @@ def tile_gnnviasmetabolicas_kernel(tc, table, w0, adj_t, b0, offs, out):
             stop=False,
         )
 
-        y_t, y_f32 = [], []
-        for mb in range(M_BLOCKS):
-            if mb % 2 == 0:
-                y_t_ps = psum.tile([P, 2 * N], BF16, name="y_t_ps", tag="bank")
+        y_t_ps = [psum.tile([P, 2 * N], BF16, name=f"y_t_ps{pair}", tag="bank") for pair in range(M_BLOCKS // 2)]
+        y_t = [held.tile([P, N], BF16, name=f"y_t{mb}") for mb in range(M_BLOCKS)]
+        y_f32 = []
+
+        def transpose(mb):
+            bank = y_t_ps[mb // 2]
             in_bank = (mb % 2) * N
             for jb in range(J_BLOCKS):
                 nc.tensor.transpose(
-                    y_t_ps[:, in_bank + jb * P : in_bank + (jb + 1) * P], y_bf16[mb][:, jb * P : (jb + 1) * P], identity[:]
+                    bank[:, in_bank + jb * P : in_bank + (jb + 1) * P], y_bf16[mb][:, jb * P : (jb + 1) * P], identity[:]
                 )
-            y_t.append(held.tile([P, N], BF16, name=f"y_t{mb}"))
-            nc.scalar.copy(y_t[mb][:], y_t_ps[:, in_bank : in_bank + N])
+            nc.scalar.copy(y_t[mb][:], bank[:, in_bank : in_bank + N])
             if mb != LAST:
                 y_f32.append(y_sb.tile([P, N], F32, name=f"y_f32_{mb}", tag="y"))
                 if mb < M_BLOCKS // 2:
@@ -86,7 +87,7 @@ def tile_gnnviasmetabolicas_kernel(tc, table, w0, adj_t, b0, offs, out):
                 else:
                     nc.scalar.copy(y_f32[mb][:], y_ps[mb][:])
 
-        for mb in range(M_BLOCKS):
+        def multiply(mb):
             sum_ps = last_sum_ps if mb == LAST else psum.tile([P, N], F32, name="sum_ps", tag="bank")
             for jb in range(J_BLOCKS):
                 nc.tensor.matmul(
@@ -108,3 +109,10 @@ def tile_gnnviasmetabolicas_kernel(tc, table, w0, adj_t, b0, offs, out):
                     nc.vector.tensor_tensor(mean[:, cols], total[:], inv_deg[:, cols], MULT)
                 nc.scalar.activation(result[:, cols], mean[:, cols], RELU, bias=b0_sb[:, mb : mb + 1])
                 nc.sync.dma_start(out_blocks[mb][:, cols], result[:, cols])
+
+        for mb in range(LAST):
+            transpose(mb)
+        multiply(0)
+        transpose(LAST)
+        for mb in range(1, M_BLOCKS):
+            multiply(mb)

@@ -3,7 +3,7 @@ from concourse.masks import make_identity
 
 BF16, F32, U16 = mybir.dt.bfloat16, mybir.dt.float32, mybir.dt.uint16
 RELU = mybir.ActivationFunctionType.Relu
-ADD, MULT = mybir.AluOpType.add, mybir.AluOpType.mult
+ADD, MULT, MAX = mybir.AluOpType.add, mybir.AluOpType.mult, mybir.AluOpType.max
 
 P = 128
 D, S, M, N = 128, 1024, 512, 512
@@ -107,7 +107,10 @@ def tile_gnnviasmetabolicas_kernel(tc, table, w0, adj_t, b0, offs, out):
                     total = work.tile([P, N // 2], F32, name="total")
                     nc.vector.tensor_tensor(total[:], sum_ps[:, cols], y_f32[mb][:, cols], ADD)
                     nc.vector.tensor_tensor(mean[:, cols], total[:], inv_deg[:, cols], MULT)
-                nc.scalar.activation(result[:, cols], mean[:, cols], RELU, bias=b0_sb[:, mb : mb + 1])
+                if mb == LAST:
+                    nc.vector.tensor_scalar(result[:, cols], mean[:, cols], b0_sb[:, mb : mb + 1], 0.0, op0=ADD, op1=MAX)
+                else:
+                    nc.scalar.activation(result[:, cols], mean[:, cols], RELU, bias=b0_sb[:, mb : mb + 1])
                 nc.sync.dma_start(out_blocks[mb][:, cols], result[:, cols])
 
         for mb in range(LAST):

@@ -2,7 +2,7 @@ import concourse.mybir as mybir
 from concourse.masks import make_identity
 
 BF16, F32, U16 = mybir.dt.bfloat16, mybir.dt.float32, mybir.dt.uint16
-RELU = mybir.ActivationFunctionType.Relu
+RELU, ABS_RSQRT = mybir.ActivationFunctionType.Relu, mybir.ActivationFunctionType.Abs_reciprocal_sqrt
 ADD, MULT, MAX = mybir.AluOpType.add, mybir.AluOpType.mult, mybir.AluOpType.max
 
 P = 128
@@ -11,6 +11,7 @@ M_BLOCKS = M // P
 J_BLOCKS = N // P
 LAST = M_BLOCKS - 1
 PSUM_BANKS = 8
+HALF = N // 2
 
 FLOPS = 2 * D * M * N + 2 * M * N * N
 
@@ -22,7 +23,7 @@ def tile_gnnviasmetabolicas_kernel(tc, table, w0, adj_t, b0, offs, out):
 
     with (
         tc.tile_pool(name="held", bufs=1) as held,
-        tc.tile_pool(name="y_sb", bufs=M_BLOCKS) as y_sb,
+        tc.tile_pool(name="rounded", bufs=2) as rounded,
         tc.tile_pool(name="work", bufs=M_BLOCKS) as work,
         tc.psum_pool(name="psum", bufs=PSUM_BANKS) as psum,
     ):
@@ -42,80 +43,105 @@ def tile_gnnviasmetabolicas_kernel(tc, table, w0, adj_t, b0, offs, out):
 
         ones = held.tile([P, P], BF16, name="ones")
         nc.vector.memset(ones[:], 1.0)
+        one = held.tile([P, 1], F32, name="one")
+        nc.vector.memset(one[:], 1.0)
         identity = held.tile([P, P], BF16, name="identity")
         make_identity(nc, identity[:])
 
         deg_ps = psum.tile([P, N], F32, name="deg_ps", tag="bank")
         for jb in range(J_BLOCKS):
             nc.tensor.matmul(deg_ps[:], ones[:], adj_sb[jb][:], start=(jb == 0), stop=(jb == J_BLOCKS - 1))
-        deg = held.tile([P, N], F32, name="deg")
-        nc.vector.tensor_scalar_add(deg[:], deg_ps[:], 1.0)
+        rsqrt = held.tile([P, N], F32, name="rsqrt")
+        nc.scalar.activation(rsqrt[:], deg_ps[:], ABS_RSQRT, bias=one[:])
         inv_deg = held.tile([P, N], F32, name="inv_deg")
-        nc.vector.reciprocal(inv_deg[:], deg[:])
+        nc.vector.tensor_tensor(inv_deg[:], rsqrt[:], rsqrt[:], MULT)
 
-        y_ps, y_bf16 = [], []
-        for mb in range(M_BLOCKS):
+        y_ps, y_f32, y_bf16 = [], {}, []
+
+        def project(mb):
             y_ps.append(psum.tile([P, N], F32, name=f"y_ps{mb}", tag="bank"))
             nc.tensor.matmul(y_ps[mb][:], w0_sb[:, mb * P : (mb + 1) * P], table_sb[:].indirect(offsets[:]))
-            y_bf16.append(y_sb.tile([P, N], BF16, name=f"y_bf16_{mb}", tag="y"))
-            nc.scalar.copy(y_bf16[mb][:], y_ps[mb][:])
-        last_sum_ps = psum.tile([P, N], F32, name="last_sum_ps", tag="bank")
-        nc.tensor.matmul(
-            last_sum_ps[:],
-            w0_sb[:, LAST * P : (LAST + 1) * P],
-            table_sb[:].indirect(offsets[:]),
-            start=True,
-            stop=False,
-        )
 
-        y_t_ps = [psum.tile([P, 2 * N], BF16, name=f"y_t_ps{pair}", tag="bank") for pair in range(M_BLOCKS // 2)]
-        y_t = [held.tile([P, N], BF16, name=f"y_t{mb}") for mb in range(M_BLOCKS)]
-        y_f32 = []
+        def copy_f32(mb):
+            y_f32[mb] = held.tile([P, N], F32, name=f"y_f32_{mb}")
+            nc.scalar.copy(y_f32[mb][:], y_ps[mb][:])
+
+        def round_bf16(mb):
+            y_bf16.append(rounded.tile([P, N], BF16, name=f"y_bf16_{mb}", tag="y_bf16"))
+            if mb == 0:
+                nc.scalar.copy(y_bf16[mb][:], y_ps[mb][:])
+            elif mb == 1:
+                nc.vector.tensor_copy(y_bf16[mb][:], y_ps[mb][:])
+            else:
+                nc.vector.tensor_copy(y_bf16[mb][:], y_f32[mb][:])
+
+        y_t = []
 
         def transpose(mb):
-            bank = y_t_ps[mb // 2]
-            in_bank = (mb % 2) * N
+            y_t_ps = psum.tile([P, N], BF16, name="y_t_ps", tag="bank")
             for jb in range(J_BLOCKS):
                 nc.tensor.transpose(
-                    bank[:, in_bank + jb * P : in_bank + (jb + 1) * P], y_bf16[mb][:, jb * P : (jb + 1) * P], identity[:]
+                    y_t_ps[:, jb * P : (jb + 1) * P], y_bf16[mb][:, jb * P : (jb + 1) * P], identity[:]
                 )
-            nc.scalar.copy(y_t[mb][:], bank[:, in_bank : in_bank + N])
-            if mb != LAST:
-                y_f32.append(y_sb.tile([P, N], F32, name=f"y_f32_{mb}", tag="y"))
-                if mb < M_BLOCKS // 2:
-                    nc.vector.tensor_copy(y_f32[mb][:], y_ps[mb][:])
-                else:
-                    nc.scalar.copy(y_f32[mb][:], y_ps[mb][:])
+            y_t.append(held.tile([P, N], BF16, name=f"y_t{mb}"))
+            if mb == 0:
+                nc.vector.tensor_copy(y_t[mb][:], y_t_ps[:])
+            else:
+                nc.scalar.copy(y_t[mb][:], y_t_ps[:])
+
+        sums = {}
 
         def multiply(mb):
-            sum_ps = last_sum_ps if mb == LAST else psum.tile([P, N], F32, name="sum_ps", tag="bank")
-            for jb in range(J_BLOCKS):
-                nc.tensor.matmul(
-                    sum_ps[:],
-                    y_t[mb][:, jb * P : (jb + 1) * P],
-                    adj_sb[jb][:],
-                    start=(jb == 0 and mb != LAST),
-                    stop=(jb == J_BLOCKS - 1),
-                )
+            width = HALF if mb == LAST else N
+            for first in range(0, N, width):
+                sum_ps = psum.tile([P, width], F32, name="sum_ps", tag="bank")
+                for jb in range(J_BLOCKS):
+                    nc.tensor.matmul(
+                        sum_ps[:],
+                        y_t[mb][:, jb * P : (jb + 1) * P],
+                        adj_sb[jb][:, first : first + width],
+                        start=(jb == 0),
+                        stop=(jb == J_BLOCKS - 1),
+                    )
+                for at in range(0, width, HALF):
+                    sums[mb, first + at] = sum_ps[:, at : at + HALF]
+
+        def finish(mb):
             mean = work.tile([P, N], F32, name="mean")
             result = work.tile([P, N], F32, name="result")
-            for half in range(2):
-                cols = slice(half * (N // 2), (half + 1) * (N // 2))
+            bias = b0_sb[:, mb : mb + 1]
+            for first in range(0, N, HALF):
+                cols = slice(first, first + HALF)
+                total = work.tile([P, HALF], F32, name="total")
+                nc.vector.tensor_tensor(total[:], sums[mb, first], y_f32[mb][:, cols], ADD)
+                nc.vector.tensor_tensor(mean[:, cols], total[:], inv_deg[:, cols], MULT)
                 if mb == LAST:
-                    nc.vector.tensor_tensor(mean[:, cols], sum_ps[:, cols], inv_deg[:, cols], MULT)
+                    nc.vector.tensor_scalar(result[:, cols], mean[:, cols], bias, 0.0, op0=ADD, op1=MAX)
                 else:
-                    total = work.tile([P, N // 2], F32, name="total")
-                    nc.vector.tensor_tensor(total[:], sum_ps[:, cols], y_f32[mb][:, cols], ADD)
-                    nc.vector.tensor_tensor(mean[:, cols], total[:], inv_deg[:, cols], MULT)
-                if mb == LAST:
-                    nc.vector.tensor_scalar(result[:, cols], mean[:, cols], b0_sb[:, mb : mb + 1], 0.0, op0=ADD, op1=MAX)
-                else:
-                    nc.scalar.activation(result[:, cols], mean[:, cols], RELU, bias=b0_sb[:, mb : mb + 1])
+                    nc.scalar.activation(result[:, cols], mean[:, cols], RELU, bias=bias)
                 nc.sync.dma_start(out_blocks[mb][:, cols], result[:, cols])
 
-        for mb in range(LAST):
-            transpose(mb)
+        project(0)
+        project(1)
+        project(2)
+        round_bf16(0)
+        round_bf16(1)
+        transpose(0)
+        copy_f32(0)
+        project(3)
+        copy_f32(2)
+        round_bf16(2)
+        transpose(1)
+        copy_f32(3)
+        round_bf16(3)
+        copy_f32(1)
         multiply(0)
-        transpose(LAST)
-        for mb in range(1, M_BLOCKS):
-            multiply(mb)
+        transpose(2)
+        multiply(1)
+        transpose(3)
+        finish(0)
+        multiply(2)
+        finish(1)
+        multiply(3)
+        finish(2)
+        finish(3)

@@ -2,7 +2,8 @@ import concourse.mybir as mybir
 from concourse.masks import make_identity
 
 BF16, F32, U16 = mybir.dt.bfloat16, mybir.dt.float32, mybir.dt.uint16
-RELU, ABS_RSQRT = mybir.ActivationFunctionType.Relu, mybir.ActivationFunctionType.Abs_reciprocal_sqrt
+RELU, SQUARE = mybir.ActivationFunctionType.Relu, mybir.ActivationFunctionType.Square
+ABS_RSQRT = mybir.ActivationFunctionType.Abs_reciprocal_sqrt
 ADD, MULT, MAX = mybir.AluOpType.add, mybir.AluOpType.mult, mybir.AluOpType.max
 
 P = 128
@@ -23,7 +24,6 @@ def tile_gnnviasmetabolicas_kernel(tc, table, w0, adj_t, b0, offs, out):
 
     with (
         tc.tile_pool(name="held", bufs=1) as held,
-        tc.tile_pool(name="rounded", bufs=2) as rounded,
         tc.tile_pool(name="work", bufs=M_BLOCKS) as work,
         tc.psum_pool(name="psum", bufs=PSUM_BANKS) as psum,
     ):
@@ -53,8 +53,6 @@ def tile_gnnviasmetabolicas_kernel(tc, table, w0, adj_t, b0, offs, out):
             nc.tensor.matmul(deg_ps[:], ones[:], adj_sb[jb][:], start=(jb == 0), stop=(jb == J_BLOCKS - 1))
         rsqrt = held.tile([P, N], F32, name="rsqrt")
         nc.scalar.activation(rsqrt[:], deg_ps[:], ABS_RSQRT, bias=one[:])
-        inv_deg = held.tile([P, N], F32, name="inv_deg")
-        nc.vector.tensor_tensor(inv_deg[:], rsqrt[:], rsqrt[:], MULT)
 
         y_ps, y_f32, y_bf16 = [], {}, []
 
@@ -63,11 +61,13 @@ def tile_gnnviasmetabolicas_kernel(tc, table, w0, adj_t, b0, offs, out):
             nc.tensor.matmul(y_ps[mb][:], w0_sb[:, mb * P : (mb + 1) * P], table_sb[:].indirect(offsets[:]))
 
         def copy_f32(mb):
-            y_f32[mb] = held.tile([P, N], F32, name=f"y_f32_{mb}")
+            slot = "rsqrt" if mb == 1 else f"y_f32_{mb}"
+            y_f32[mb] = held.tile([P, N], F32, name=f"y_f32_{mb}", tag=slot)
             nc.scalar.copy(y_f32[mb][:], y_ps[mb][:])
 
         def round_bf16(mb):
-            y_bf16.append(rounded.tile([P, N], BF16, name=f"y_bf16_{mb}", tag="y_bf16"))
+            slot = 0 if mb == 2 else mb
+            y_bf16.append(held.tile([P, N], BF16, name=f"y_bf16_{mb}", tag=f"y_bf16_{slot}"))
             if mb == 0:
                 nc.scalar.copy(y_bf16[mb][:], y_ps[mb][:])
             elif mb == 1:
@@ -84,7 +84,7 @@ def tile_gnnviasmetabolicas_kernel(tc, table, w0, adj_t, b0, offs, out):
                     y_t_ps[:, jb * P : (jb + 1) * P], y_bf16[mb][:, jb * P : (jb + 1) * P], identity[:]
                 )
             y_t.append(held.tile([P, N], BF16, name=f"y_t{mb}"))
-            if mb == 0:
+            if mb != LAST:
                 nc.vector.tensor_copy(y_t[mb][:], y_t_ps[:])
             else:
                 nc.scalar.copy(y_t[mb][:], y_t_ps[:])
@@ -108,7 +108,7 @@ def tile_gnnviasmetabolicas_kernel(tc, table, w0, adj_t, b0, offs, out):
 
         def finish(mb):
             mean = work.tile([P, N], F32, name="mean")
-            result = work.tile([P, N], F32, name="result")
+            result = held.tile([P, N], F32, name=f"result{mb}", tag=f"y_bf16_{LAST}" if mb == 0 else f"result{mb}")
             bias = b0_sb[:, mb : mb + 1]
             for first in range(0, N, HALF):
                 cols = slice(first, first + HALF)
@@ -134,6 +134,10 @@ def tile_gnnviasmetabolicas_kernel(tc, table, w0, adj_t, b0, offs, out):
         transpose(1)
         copy_f32(3)
         round_bf16(3)
+
+        inv_deg = held.tile([P, N], F32, name="inv_deg", tag="y_bf16_1")
+        nc.scalar.activation(inv_deg[:], rsqrt[:], SQUARE)
+
         copy_f32(1)
         multiply(0)
         transpose(2)

@@ -27,16 +27,16 @@ def tile_gnnviasmetabolicas_kernel(tc, table, w0, adj_t, b0, offs, out):
         tc.tile_pool(name="work", bufs=M_BLOCKS) as work,
         tc.psum_pool(name="psum", bufs=PSUM_BANKS) as psum,
     ):
-        adj_sb = [held.tile([P, N], BF16, name=f"adj_sb{jb}") for jb in range(J_BLOCKS)]
-        for jb in range(J_BLOCKS):
-            queue = nc.sync if jb % 2 == 0 else nc.scalar
-            queue.dma_start(adj_sb[jb][:], adj_blocks[jb])
         offsets = held.tile([P, N // 16], U16, name="offsets")
         nc.sync.dma_start(offsets[:], offs)
         table_sb = held.tile([P, S], BF16, name="table_sb")
         nc.sync.dma_start(table_sb[:], table)
         w0_sb = held.tile([P, M], BF16, name="w0_sb")
         nc.scalar.dma_start(w0_sb[:], w0)
+        adj_sb = [held.tile([P, N], BF16, name=f"adj_sb{jb}") for jb in range(J_BLOCKS)]
+        for jb in range(J_BLOCKS):
+            queue = nc.scalar if jb % 2 == 0 else nc.sync
+            queue.dma_start(adj_sb[jb][:], adj_blocks[jb])
         b0_sb = held.tile([P, M_BLOCKS], F32, name="b0_sb")
         with nc.allow_non_contiguous_dma(reason="512 floats, one to a partition and block"):
             nc.sync.dma_start(b0_sb[:], b0.rearrange("(mb p) one -> p (mb one)", p=P))
@@ -47,12 +47,6 @@ def tile_gnnviasmetabolicas_kernel(tc, table, w0, adj_t, b0, offs, out):
         nc.vector.memset(one[:], 1.0)
         identity = held.tile([P, P], BF16, name="identity")
         make_identity(nc, identity[:])
-
-        deg_ps = psum.tile([P, N], F32, name="deg_ps", tag="bank")
-        for jb in range(J_BLOCKS):
-            nc.tensor.matmul(deg_ps[:], ones[:], adj_sb[jb][:], start=(jb == 0), stop=(jb == J_BLOCKS - 1))
-        rsqrt = held.tile([P, N], F32, name="rsqrt")
-        nc.scalar.activation(rsqrt[:], deg_ps[:], ABS_RSQRT, bias=one[:])
 
         y_ps, y_f32, y_bf16 = [], {}, []
 
@@ -129,6 +123,13 @@ def tile_gnnviasmetabolicas_kernel(tc, table, w0, adj_t, b0, offs, out):
         transpose(0)
         copy_f32(0)
         project(3)
+
+        deg_ps = psum.tile([P, N], F32, name="deg_ps", tag="bank")
+        for jb in range(J_BLOCKS):
+            nc.tensor.matmul(deg_ps[:], ones[:], adj_sb[jb][:], start=(jb == 0), stop=(jb == J_BLOCKS - 1))
+        rsqrt = held.tile([P, N], F32, name="rsqrt")
+        nc.scalar.activation(rsqrt[:], deg_ps[:], ABS_RSQRT, bias=one[:])
+
         copy_f32(2)
         round_bf16(2)
         transpose(1)

@@ -45,6 +45,8 @@ def tile_gnnviasmetabolicas_kernel(tc, table, w0, adj_t, b0, offs, out):
         nc.vector.memset(ones[:], 1.0)
         one = held.tile([P, 1], F32, name="one")
         nc.vector.memset(one[:], 1.0)
+        first_call = held.tile([P, 1], F32, name="first_call")
+        nc.scalar.activation(first_call[:], one[:], ABS_RSQRT, bias=one[:])
         identity = held.tile([P, P], BF16, name="identity")
         make_identity(nc, identity[:])
 

@@ -29,14 +29,14 @@ def tile_gnnviasmetabolicas_kernel(tc, table, w0, adj_t, b0, offs, out):
     ):
         offsets = held.tile([P, N // 16], U16, name="offsets")
         nc.sync.dma_start(offsets[:], offs)
+        w0_sb = held.tile([P, M], BF16, name="w0_sb")
+        nc.sync.dma_start(w0_sb[:, :P], w0[:, :P])
         table_sb = held.tile([P, S], BF16, name="table_sb")
         nc.sync.dma_start(table_sb[:], table)
-        w0_sb = held.tile([P, M], BF16, name="w0_sb")
-        nc.scalar.dma_start(w0_sb[:], w0)
+        nc.sync.dma_start(w0_sb[:, P:], w0[:, P:])
         adj_sb = [held.tile([P, N], BF16, name=f"adj_sb{jb}") for jb in range(J_BLOCKS)]
         for jb in range(J_BLOCKS):
-            queue = nc.scalar if jb % 2 == 0 else nc.sync
-            queue.dma_start(adj_sb[jb][:], adj_blocks[jb])
+            nc.sync.dma_start(adj_sb[jb][:], adj_blocks[jb])
         b0_sb = held.tile([P, M_BLOCKS], F32, name="b0_sb")
         with nc.allow_non_contiguous_dma(reason="512 floats, one to a partition and block"):
             nc.sync.dma_start(b0_sb[:], b0.rearrange("(mb p) one -> p (mb one)", p=P))

@@ -115,7 +115,10 @@ def tile_gnnviasmetabolicas_kernel(tc, table, w0, adj_t, b0, offs, out):
                     nc.vector.tensor_scalar(result[:, cols], mean[:, cols], bias, 0.0, op0=ADD, op1=MAX)
                 else:
                     nc.scalar.activation(result[:, cols], mean[:, cols], RELU, bias=bias)
-                nc.sync.dma_start(out_blocks[mb][:, cols], result[:, cols])
+                if mb == LAST:
+                    nc.sync.dma_start(out_blocks[mb][:, cols], result[:, cols])
+            if mb != LAST:
+                nc.sync.dma_start(out_blocks[mb], result[:])
 
         project(0)
         project(1)
@@ -142,10 +145,10 @@ def tile_gnnviasmetabolicas_kernel(tc, table, w0, adj_t, b0, offs, out):
         nc.scalar.activation(inv_deg[:], rsqrt[:], SQUARE)
 
         copy_f32(1)
-        multiply(0)
         transpose(2)
-        multiply(1)
+        multiply(0)
         transpose(3)
+        multiply(1)
         finish(0)
         multiply(2)
         finish(1)

@@ -3,7 +3,7 @@ from concourse.masks import make_identity
 
 BF16, F32, U16 = mybir.dt.bfloat16, mybir.dt.float32, mybir.dt.uint16
 RELU, SQUARE = mybir.ActivationFunctionType.Relu, mybir.ActivationFunctionType.Square
-ABS_RSQRT = mybir.ActivationFunctionType.Abs_reciprocal_sqrt
+IDENTITY, ABS_RSQRT = mybir.ActivationFunctionType.Identity, mybir.ActivationFunctionType.Abs_reciprocal_sqrt
 ADD, MULT, MAX = mybir.AluOpType.add, mybir.AluOpType.mult, mybir.AluOpType.max
 
 P = 128
@@ -59,17 +59,20 @@ def tile_gnnviasmetabolicas_kernel(tc, table, w0, adj_t, b0, offs, out):
         def copy_f32(mb):
             slot = "rsqrt" if mb == 1 else f"y_f32_{mb}"
             y_f32[mb] = held.tile([P, N], F32, name=f"y_f32_{mb}", tag=slot)
-            nc.scalar.copy(y_f32[mb][:], y_ps[mb][:])
+            if mb == LAST:
+                nc.scalar.activation(y_f32[mb][:], y_ps[mb][:], IDENTITY, bias=b0_sb[:, LAST:])
+            else:
+                nc.scalar.copy(y_f32[mb][:], y_ps[mb][:])
 
         def round_bf16(mb):
             slot = 0 if mb == 2 else mb
             y_bf16.append(held.tile([P, N], BF16, name=f"y_bf16_{mb}", tag=f"y_bf16_{slot}"))
             if mb == 0:
                 nc.scalar.copy(y_bf16[mb][:], y_ps[mb][:])
-            elif mb == 1:
-                nc.vector.tensor_copy(y_bf16[mb][:], y_ps[mb][:])
-            else:
+            elif mb == 2:
                 nc.vector.tensor_copy(y_bf16[mb][:], y_f32[mb][:])
+            else:
+                nc.vector.tensor_copy(y_bf16[mb][:], y_ps[mb][:])
 
         y_t = []
 
@@ -103,21 +106,24 @@ def tile_gnnviasmetabolicas_kernel(tc, table, w0, adj_t, b0, offs, out):
                     sums[mb, first + at] = sum_ps[:, at : at + HALF]
 
         def finish(mb):
-            mean = work.tile([P, N], F32, name="mean")
+            mean = work.tile([P, N], F32, name="mean") if mb != LAST else None
             result = held.tile([P, N], F32, name=f"result{mb}", tag=f"y_bf16_{LAST}" if mb == 0 else f"result{mb}")
             bias = b0_sb[:, mb : mb + 1]
             for first in range(0, N, HALF):
                 cols = slice(first, first + HALF)
                 total = work.tile([P, HALF], F32, name="total")
-                nc.vector.tensor_tensor(total[:], sums[mb, first], y_f32[mb][:, cols], ADD)
-                nc.vector.tensor_tensor(mean[:, cols], total[:], inv_deg[:, cols], MULT)
                 if mb == LAST:
-                    nc.vector.tensor_scalar(result[:, cols], mean[:, cols], bias, 0.0, op0=ADD, op1=MAX)
+                    nc.vector.tensor_tensor(total[:], sums[mb, first], lifted[:, cols], ADD)
+                    nc.vector.scalar_tensor_tensor(
+                        result[:, cols], total[:], 0.0, inv_deg[:, cols], op0=MAX, op1=MULT
+                    )
                 else:
+                    nc.vector.tensor_tensor(total[:], sums[mb, first], y_f32[mb][:, cols], ADD)
+                    nc.vector.tensor_tensor(mean[:, cols], total[:], inv_deg[:, cols], MULT)
                     nc.scalar.activation(result[:, cols], mean[:, cols], RELU, bias=bias)
-                if mb == LAST:
+                if mb >= LAST - 1:
                     nc.sync.dma_start(out_blocks[mb][:, cols], result[:, cols])
-            if mb != LAST:
+            if mb < LAST - 1:
                 nc.sync.dma_start(out_blocks[mb], result[:])
 
         project(0)
@@ -146,6 +152,12 @@ def tile_gnnviasmetabolicas_kernel(tc, table, w0, adj_t, b0, offs, out):
 
         copy_f32(1)
         transpose(2)
+
+        lifted = held.tile([P, N], F32, name="lifted", tag="y_bf16_0")
+        nc.vector.scalar_tensor_tensor(
+            lifted[:], deg_ps[:], b0_sb[:, LAST:], y_f32[LAST][:], op0=MULT, op1=ADD
+        )
+
         multiply(0)
         transpose(3)
         multiply(1)

@@ -119,7 +119,8 @@ def tile_gnnviasmetabolicas_kernel(tc, table, w0, adj_t, b0, offs, out):
                     )
                 else:
                     nc.vector.tensor_tensor(total[:], sums[mb, first], y_f32[mb][:, cols], ADD)
-                    nc.vector.tensor_tensor(mean[:, cols], total[:], inv_deg[:, cols], MULT)
+                    divider = nc.gpsimd if mb < LAST - 1 and first == HALF else nc.vector
+                    divider.tensor_tensor(mean[:, cols], total[:], inv_deg[:, cols], MULT)
                     nc.scalar.activation(result[:, cols], mean[:, cols], RELU, bias=bias)
                 if mb >= LAST - 1:
                     nc.sync.dma_start(out_blocks[mb][:, cols], result[:, cols])

@@ -27,12 +27,12 @@ def tile_gnnviasmetabolicas_kernel(tc, table, w0, adj_t, b0, offs, out):
         tc.tile_pool(name="work", bufs=M_BLOCKS) as work,
         tc.psum_pool(name="psum", bufs=PSUM_BANKS) as psum,
     ):
+        table_sb = held.tile([P, S], BF16, name="table_sb")
+        nc.sync.dma_start(table_sb[:], table)
         offsets = held.tile([P, N // 16], U16, name="offsets")
         nc.sync.dma_start(offsets[:], offs)
         w0_sb = held.tile([P, M], BF16, name="w0_sb")
         nc.sync.dma_start(w0_sb[:, :P], w0[:, :P])
-        table_sb = held.tile([P, S], BF16, name="table_sb")
-        nc.sync.dma_start(table_sb[:], table)
         nc.sync.dma_start(w0_sb[:, P:], w0[:, P:])
         adj_sb = [held.tile([P, N], BF16, name=f"adj_sb{jb}") for jb in range(J_BLOCKS)]
         for jb in range(J_BLOCKS):
@@ -122,9 +122,9 @@ def tile_gnnviasmetabolicas_kernel(tc, table, w0, adj_t, b0, offs, out):
                     divider = nc.gpsimd if mb < LAST - 1 and first == HALF else nc.vector
                     divider.tensor_tensor(mean[:, cols], total[:], inv_deg[:, cols], MULT)
                     nc.scalar.activation(result[:, cols], mean[:, cols], RELU, bias=bias)
-                if mb >= LAST - 1:
+                if mb > 0:
                     nc.sync.dma_start(out_blocks[mb][:, cols], result[:, cols])
-            if mb < LAST - 1:
+            if mb == 0:
                 nc.sync.dma_start(out_blocks[mb], result[:])
 
         project(0)

import concourse.mybir as mybir
from concourse.masks import make_identity

BF16, F32, U16 = mybir.dt.bfloat16, mybir.dt.float32, mybir.dt.uint16
RELU, SQUARE = mybir.ActivationFunctionType.Relu, mybir.ActivationFunctionType.Square
IDENTITY, ABS_RSQRT = mybir.ActivationFunctionType.Identity, mybir.ActivationFunctionType.Abs_reciprocal_sqrt
ADD, MULT, MAX = mybir.AluOpType.add, mybir.AluOpType.mult, mybir.AluOpType.max

P = 128
D, S, M, N = 128, 1024, 512, 512
M_BLOCKS = M // P
J_BLOCKS = N // P
LAST = M_BLOCKS - 1
PSUM_BANKS = 8
HALF = N // 2

FLOPS = 2 * D * M * N + 2 * M * N * N


def tile_gnnviasmetabolicas_kernel(tc, table, w0, adj_t, b0, offs, out):
    nc = tc.nc
    adj_blocks = adj_t.rearrange("(jb p) i -> jb p i", p=P)
    out_blocks = out.rearrange("(mb p) i -> mb p i", p=P)

    with (
        tc.tile_pool(name="held", bufs=1) as held,
        tc.tile_pool(name="work", bufs=M_BLOCKS) as work,
        tc.psum_pool(name="psum", bufs=PSUM_BANKS) as psum,
    ):
        table_sb = held.tile([P, S], BF16, name="table_sb")
        nc.sync.dma_start(table_sb[:], table)
        offsets = held.tile([P, N // 16], U16, name="offsets")
        nc.sync.dma_start(offsets[:], offs)
        w0_sb = held.tile([P, M], BF16, name="w0_sb")
        nc.sync.dma_start(w0_sb[:, :P], w0[:, :P])
        nc.sync.dma_start(w0_sb[:, P:], w0[:, P:])
        adj_sb = [held.tile([P, N], BF16, name=f"adj_sb{jb}") for jb in range(J_BLOCKS)]
        for jb in range(J_BLOCKS):
            nc.sync.dma_start(adj_sb[jb][:], adj_blocks[jb])
        b0_sb = held.tile([P, M_BLOCKS], F32, name="b0_sb")
        with nc.allow_non_contiguous_dma(reason="512 floats, one to a partition and block"):
            nc.sync.dma_start(b0_sb[:], b0.rearrange("(mb p) one -> p (mb one)", p=P))

        ones = held.tile([P, P], BF16, name="ones")
        nc.vector.memset(ones[:], 1.0)
        one = held.tile([P, 1], F32, name="one")
        nc.vector.memset(one[:], 1.0)
        first_call = held.tile([P, 1], F32, name="first_call")
        nc.scalar.activation(first_call[:], one[:], ABS_RSQRT, bias=one[:])
        identity = held.tile([P, P], BF16, name="identity")
        make_identity(nc, identity[:])

        y_ps, y_f32, y_bf16 = [], {}, []

        def project(mb):
            y_ps.append(psum.tile([P, N], F32, name=f"y_ps{mb}", tag="bank"))
            nc.tensor.matmul(y_ps[mb][:], w0_sb[:, mb * P : (mb + 1) * P], table_sb[:].indirect(offsets[:]))

        def copy_f32(mb):
            slot = "rsqrt" if mb == 1 else f"y_f32_{mb}"
            y_f32[mb] = held.tile([P, N], F32, name=f"y_f32_{mb}", tag=slot)
            if mb == LAST:
                nc.scalar.activation(y_f32[mb][:], y_ps[mb][:], IDENTITY, bias=b0_sb[:, LAST:])
            else:
                nc.scalar.copy(y_f32[mb][:], y_ps[mb][:])

        def round_bf16(mb):
            slot = 0 if mb == 2 else mb
            y_bf16.append(held.tile([P, N], BF16, name=f"y_bf16_{mb}", tag=f"y_bf16_{slot}"))
            if mb == 0:
                nc.scalar.copy(y_bf16[mb][:], y_ps[mb][:])
            elif mb == 2:
                nc.vector.tensor_copy(y_bf16[mb][:], y_f32[mb][:])
            else:
                nc.vector.tensor_copy(y_bf16[mb][:], y_ps[mb][:])

        y_t = []

        def transpose(mb):
            y_t_ps = psum.tile([P, N], BF16, name="y_t_ps", tag="bank")
            for jb in range(J_BLOCKS):
                nc.tensor.transpose(
                    y_t_ps[:, jb * P : (jb + 1) * P], y_bf16[mb][:, jb * P : (jb + 1) * P], identity[:]
                )
            y_t.append(held.tile([P, N], BF16, name=f"y_t{mb}"))
            if mb != LAST:
                nc.vector.tensor_copy(y_t[mb][:], y_t_ps[:])
            else:
                nc.scalar.copy(y_t[mb][:], y_t_ps[:])

        sums = {}

        def multiply(mb):
            width = HALF if mb == LAST else N
            for first in range(0, N, width):
                sum_ps = psum.tile([P, width], F32, name="sum_ps", tag="bank")
                for jb in range(J_BLOCKS):
                    nc.tensor.matmul(
                        sum_ps[:],
                        y_t[mb][:, jb * P : (jb + 1) * P],
                        adj_sb[jb][:, first : first + width],
                        start=(jb == 0),
                        stop=(jb == J_BLOCKS - 1),
                    )
                for at in range(0, width, HALF):
                    sums[mb, first + at] = sum_ps[:, at : at + HALF]

        def finish(mb):
            mean = work.tile([P, N], F32, name="mean") if mb != LAST else None
            result = held.tile([P, N], F32, name=f"result{mb}", tag=f"y_bf16_{LAST}" if mb == 0 else f"result{mb}")
            bias = b0_sb[:, mb : mb + 1]
            for first in range(0, N, HALF):
                cols = slice(first, first + HALF)
                total = work.tile([P, HALF], F32, name="total")
                if mb == LAST:
                    nc.vector.tensor_tensor(total[:], sums[mb, first], lifted[:, cols], ADD)
                    nc.vector.scalar_tensor_tensor(
                        result[:, cols], total[:], 0.0, inv_deg[:, cols], op0=MAX, op1=MULT
                    )
                else:
                    nc.vector.tensor_tensor(total[:], sums[mb, first], y_f32[mb][:, cols], ADD)
                    divider = nc.gpsimd if mb < LAST - 1 and first == HALF else nc.vector
                    divider.tensor_tensor(mean[:, cols], total[:], inv_deg[:, cols], MULT)
                    nc.scalar.activation(result[:, cols], mean[:, cols], RELU, bias=bias)
                if mb > 0:
                    nc.sync.dma_start(out_blocks[mb][:, cols], result[:, cols])
            if mb == 0:
                nc.sync.dma_start(out_blocks[mb], result[:])

        project(0)
        project(1)
        project(2)
        round_bf16(0)
        round_bf16(1)
        transpose(0)
        copy_f32(0)
        project(3)

        deg_ps = psum.tile([P, N], F32, name="deg_ps", tag="bank")
        for jb in range(J_BLOCKS):
            nc.tensor.matmul(deg_ps[:], ones[:], adj_sb[jb][:], start=(jb == 0), stop=(jb == J_BLOCKS - 1))
        rsqrt = held.tile([P, N], F32, name="rsqrt")
        nc.scalar.activation(rsqrt[:], deg_ps[:], ABS_RSQRT, bias=one[:])

        copy_f32(2)
        round_bf16(2)
        transpose(1)
        copy_f32(3)
        round_bf16(3)

        inv_deg = held.tile([P, N], F32, name="inv_deg", tag="y_bf16_1")
        nc.scalar.activation(inv_deg[:], rsqrt[:], SQUARE)

        copy_f32(1)
        transpose(2)

        lifted = held.tile([P, N], F32, name="lifted", tag="y_bf16_0")
        nc.vector.scalar_tensor_tensor(
            lifted[:], deg_ps[:], b0_sb[:, LAST:], y_f32[LAST][:], op0=MULT, op1=ADD
        )

        multiply(0)
        transpose(3)
        multiply(1)
        finish(0)
        multiply(2)
        finish(1)
        multiply(3)
        finish(2)
        finish(3)
